import numpy as np
import ml_dtypes


def mxq(x, axis, fmt="e4m3"):
    dtype, down = {"e4m3": (ml_dtypes.float8_e4m3fn, 7), "e5m2": (ml_dtypes.float8_e5m2, 14)}[fmt]
    v = np.moveaxis(np.asarray(x, np.float32).astype(ml_dtypes.bfloat16).astype(np.float64), axis, -1)
    blocks = v.reshape(v.shape[:-1] + (-1, 32))
    amax = np.abs(blocks).max(-1, keepdims=True)
    byte = np.maximum(np.where(amax > 0, np.frexp(amax)[1] - 1 + 127, 0) - down, 1)
    scale = np.exp2(byte - 127.0)
    codes = (blocks / scale).astype(np.float32).astype(dtype).astype(np.float64)
    return np.moveaxis((codes * scale).reshape(v.shape), -1, axis)


WIDE = False


def mx_kscale(k):
    if not WIDE:
        return np.ones(k)
    levels = np.array([10, -10, 5, -5, 0])
    if k % 512:
        return np.exp2(np.random.permutation(np.resize(levels, k // 32))).repeat(32)
    a = np.empty((k // 512, 16))
    for p in range(k // 512):
        a[p, :8] = np.random.permutation(np.resize(levels, 8))
        for g in range(8):
            far = levels[np.abs(levels - a[p, g]) >= 10]
            a[p, g + 8] = far[np.random.randint(len(far))]
    return np.exp2(a.ravel()).repeat(32)


BF16 = ml_dtypes.bfloat16


def bf(x):
    return np.asarray(x, np.float32).astype(BF16)


def f64(x):
    return np.asarray(x).astype(np.float64)


P, N, Z, H1, H2, C = 8, 128, 16, 8192, 128, 256
EPS = 1e-5


def batch_norm(h, gamma, beta):
    mu = h.mean(axis=1, keepdims=True)
    var = h.var(axis=1, keepdims=True)
    return (h - mu) * (1.0 / np.sqrt(var + EPS)) * gamma[:, None, :] + beta[:, None, :]


def setup_inputs():
    r = np.random.standard_normal
    t = mx_kscale(H1)
    sd = np.where(np.random.random((P, 1, H1)) < 0.25, np.sqrt(EPS), 1.0)
    return {"h6_pre": bf((r((P, N, H1)) + 0.5 * r((P, 1, H1))) * sd),
            "g6": bf((1.0 + 0.1 * r((P, H1))) * t),
            "be6": bf(0.3 * r((P, H1)) * t),
            "W7": bf(r((P, H2, H1)) / np.sqrt(H1) / t),
            "b7": bf(0.3 * r((P, H2)))}


def reference(h6_pre, g6, be6, W7, b7):
    a = np.maximum(batch_norm(f64(h6_pre), f64(g6), f64(be6)), 0.0)
    y = mxq(a, 2, "e4m3") @ mxq(f64(W7), 2, "e4m3").transpose(0, 2, 1)
    return y + f64(b7)[:, None, :]

@@ -1,0 +1,300 @@
+from contextlib import ExitStack
+
+import concourse.mybir as mybir
+from concourse.masks import make_identity
+
+F32 = mybir.dt.float32
+BF16 = mybir.dt.bfloat16
+U32 = mybir.dt.uint32
+U8 = mybir.dt.uint8
+FP8X4 = mybir.dt.float8_e4m3fn_x4
+ACT = mybir.ActivationFunctionType
+ALU = mybir.AluOpType
+
+P = 128
+BLOCKS = 8
+ROWS = 128
+FEATS = 8192
+OUTS = 128
+EPS = 1e-5
+
+PACK = 4
+PAIR = 2
+GROUP_K = P * PAIR
+K_PASS = P * PACK
+PASSES = FEATS // K_PASS
+BANK_GROUPS = 4
+BANK_PASSES = 2
+BANK_COLS = BANK_PASSES * ROWS
+BATCH_BANKS = 2
+BATCH_K = BATCH_BANKS * BANK_GROUPS * GROUP_K
+BATCH_GROUPS = BATCH_BANKS * BANK_GROUPS
+BATCH_FEATS = BATCH_GROUPS * PAIR
+BATCH_PASSES = BATCH_BANKS * BANK_PASSES
+BATCH_COLS = BATCH_BANKS * BANK_COLS
+BLOCK_BATCHES = FEATS // BATCH_K
+BATCHES = BLOCKS * BLOCK_BATCHES
+RUN = 4
+A_LAG = 3
+PREFETCH = 6
+
+FLOPS = 2 * BLOCKS * ROWS * OUTS * FEATS
+
+
+def tile_decoder_pa_k_kernel(tc, h6_pre, g6, be6, W7, b7, out):
+    nc = tc.nc
+    with ExitStack() as ctx:
+        const = ctx.enter_context(tc.tile_pool(name="const", bufs=1))
+        rows_pool = ctx.enter_context(tc.tile_pool(name="rows_pool", bufs=PREFETCH + 2))
+        block_pool = ctx.enter_context(tc.tile_pool(name="block_pool", bufs=2))
+        work = ctx.enter_context(tc.tile_pool(name="work", bufs=3))
+        ps_h = ctx.enter_context(tc.psum_pool(name="ps_h", bufs=3 * BATCH_BANKS))
+        ps_w = ctx.enter_context(tc.psum_pool(name="ps_w", bufs=1))
+        ps_acc = ctx.enter_context(tc.psum_pool(name="ps_acc", bufs=1))
+
+        ident = const.tile([P, P], F32)
+        make_identity(nc, ident[:])
+        zero_col = const.tile([P, 1], F32)
+        nc.vector.memset(zero_col[:], 0.0)
+        eps_col = const.tile([P, 1], F32)
+        nc.vector.tensor_scalar(out=eps_col[:], in0=zero_col[:], scalar1=1.0, scalar2=EPS, op0=ALU.mult, op1=ALU.add)
+
+        def transpose_bank(bank, rows_tile, ci):
+            words = rows_tile[:].bitcast(F32)
+            for g in range(BANK_PASSES):
+                for u in range(PAIR):
+                    first = (BANK_PASSES * ci + g) * GROUP_K
+                    quarter = BANK_PASSES * u + g
+                    nc.tensor.transpose(
+                        bank[:, quarter * P : (quarter + 1) * P], words[:, first + u : first + GROUP_K : PAIR], ident[:]
+                    )
+
+        affine_ps = ps_h.tile([P, BANK_GROUPS * P], F32, tag="h_ps")
+        for v, vec in enumerate((g6, be6)):
+            vec_rows = const.tile([P, K_PASS], BF16, name="vec_rows%d" % v)
+            nc.scalar.dma_start(out=vec_rows[:], in_=vec.rearrange("b (s w) -> (b s) w", w=K_PASS))
+            for u in range(PAIR):
+                quarter = PAIR * v + u
+                nc.tensor.transpose(
+                    affine_ps[:, quarter * P : (quarter + 1) * P], vec_rows[:].bitcast(F32)[:, u::PAIR], ident[:]
+                )
+        affine = const.tile([P, 2, BATCHES * BATCH_FEATS], F32)
+        for v in range(2):
+            nc.vector.tensor_copy(
+                out=affine[:, v, :].rearrange("p (s u e) -> p s u e", u=PAIR, e=PAIR),
+                in_=affine_ps[:].bitcast(BF16).rearrange("p (v u s e) -> p v s u e", v=2, u=PAIR, e=PAIR)[:, v],
+            )
+
+        bias_all = const.tile([P, BLOCKS * OUTS], BF16)
+
+        h_rows = {}
+        w_rows = {}
+        h_banks = {}
+        w_banks = {}
+        stats = {}
+        stds = {}
+        gain_means = {}
+        rstds = {}
+        means_scaled = {}
+        scales = {}
+        shifts = {}
+        a_planes = {}
+        a_grouped = {}
+        w_grouped = {}
+        a_mx = {}
+        w_mx = {}
+        accs = {}
+
+        def batch_feats(t):
+            return slice(t * BATCH_FEATS, (t + 1) * BATCH_FEATS)
+
+        def load(t):
+            b, r = divmod(t, BLOCK_BATCHES)
+            feats = slice(r * BATCH_K, (r + 1) * BATCH_K)
+            h_tile = rows_pool.tile([P, BATCH_K], BF16)
+            nc.sync.dma_start(out=h_tile[:], in_=h6_pre[b][:, feats])
+            w_tile = rows_pool.tile([P, BATCH_K], BF16)
+            nc.sync.dma_start(out=w_tile[:], in_=W7[b][:, feats])
+            h_rows[t] = h_tile
+            w_rows[t] = w_tile
+
+        def transpose_h(t, ci):
+            h_ps = ps_h.tile([P, BANK_GROUPS * P], F32)
+            transpose_bank(h_ps, h_rows[t], ci)
+            h_banks[t, ci] = h_ps
+
+        def statistics(t):
+            batch_stats = work.tile([P, BATCH_GROUPS, 6], F32)
+            for ci in range(BATCH_BANKS):
+                for g in range(BANK_PASSES):
+                    for u in range(PAIR):
+                        quarter = BANK_PASSES * u + g
+                        nc.vector.bn_stats(
+                            out=batch_stats[:, BANK_GROUPS * ci + PAIR * g + u, :],
+                            in_=h_banks[t, ci][:, quarter * P : (quarter + 1) * P].bitcast(BF16),
+                        )
+            stats[t] = batch_stats[:].rearrange("p i (e s) -> p s (i e)", s=3)
+
+        def spread(t):
+            std = work.tile([P, BATCH_FEATS], F32)
+            nc.scalar.activation(out=std[:], in_=stats[t][:, 2, :], func=ACT.Sqrt, scale=1.0 / ROWS, bias=eps_col[:])
+            stds[t] = std
+
+        def gain_times_mean(t):
+            gain_mean = work.tile([P, BATCH_FEATS], F32)
+            nc.vector.tensor_mul(out=gain_mean[:], in0=stats[t][:, 1, :], in1=affine[:, 0, batch_feats(t)])
+            gain_means[t] = gain_mean
+
+        def inverse_spread(t):
+            rstd = work.tile([P, BATCH_FEATS], F32)
+            nc.vector.reciprocal(out=rstd[:], in_=stds[t][:])
+            rstds[t] = rstd
+
+        def scale_terms(t):
+            scale = work.tile([P, BATCH_FEATS], F32)
+            nc.vector.tensor_mul(out=scale[:], in0=rstds[t][:], in1=affine[:, 0, batch_feats(t)])
+            mean_scaled = work.tile([P, BATCH_FEATS], F32)
+            nc.vector.tensor_mul(out=mean_scaled[:], in0=rstds[t][:], in1=gain_means[t][:])
+            scales[t] = scale
+            means_scaled[t] = mean_scaled
+
+        def shift_term(t):
+            shift = work.tile([P, BATCH_FEATS], F32)
+            nc.vector.tensor_sub(out=shift[:], in0=affine[:, 1, batch_feats(t)], in1=means_scaled[t][:])
+            shifts[t] = shift
+
+        def activations(t, ci, g):
+            if ci == 0 and g == 0:
+                planes_tile = work.tile([P, PACK, BATCH_COLS], BF16)
+                a_planes[t] = planes_tile
+            halves = h_banks[t, ci][:].bitcast(BF16).rearrange(
+                "p (u g n e) -> p u g n e", u=PAIR, g=BANK_PASSES, e=PAIR
+            )
+            first = ci * BANK_COLS + g * ROWS
+            for u in range(PAIR):
+                for e in range(PAIR):
+                    col = PAIR * (BANK_GROUPS * ci + PAIR * g + u) + e
+                    nc.scalar.activation(
+                        out=a_planes[t][:, PAIR * u + e, first : first + ROWS],
+                        in_=halves[:, u, g, :, e],
+                        func=ACT.Relu,
+                        scale=scales[t][:, col : col + 1],
+                        bias=shifts[t][:, col : col + 1],
+                    )
+
+        def regroup(t):
+            grouped_tile = work.tile([P, BATCH_COLS, PACK], BF16, name="a_grouped", align_bytes=64)
+            nc.gpsimd.tensor_scalar(
+                out=grouped_tile[:].rearrange("p (c i) t -> p c t i", i=RUN),
+                in0=a_planes[t][:].rearrange("p t (c i) -> p c t i", i=RUN),
+                scalar1=1.0,
+                scalar2=0.0,
+                op0=ALU.mult,
+                op1=ALU.add,
+            )
+            a_grouped[t] = grouped_tile
+
+        def transpose_w(t, ci):
+            w_ps = ps_w.tile([P, BANK_GROUPS * P], F32)
+            transpose_bank(w_ps, w_rows[t], ci)
+            w_banks[t, ci] = w_ps
+
+        def copy_w(t, ci):
+            if ci == 0:
+                grouped_tile = work.tile([P, BATCH_COLS, PACK], BF16, name="w_grouped", align_bytes=64)
+                w_grouped[t] = grouped_tile
+            part = w_grouped[t][:, ci * BANK_COLS : (ci + 1) * BANK_COLS, :]
+            nc.scalar.copy(
+                out=part.rearrange("p m t -> p (m t)").bitcast(F32).rearrange("p (m u) -> p m u", u=PAIR),
+                in_=w_banks[t, ci][:].rearrange("p (u m) -> p m u", u=PAIR),
+            )
+
+        def quantise(grouped, mx, name, t, ci):
+            b, r = divmod(t, BLOCK_BATCHES)
+            if r == 0 and ci == 0:
+                codes_tile = block_pool.tile([P, PASSES * P], U32, name=name + "_codes", align_bytes=64)
+                scale_bytes = block_pool.tile([P, PASSES * P], U8, name=name + "_scale_bytes", align_bytes=64)
+                mx[b] = (codes_tile, scale_bytes)
+            codes_tile, scale_bytes = mx[b]
+            first = r * BATCH_COLS + ci * BANK_COLS
+            cols = slice(first, first + BANK_COLS)
+            nc.vector.quantize_mx(
+                out=codes_tile[:, cols].bitcast(FP8X4),
+                scales=scale_bytes[:, cols],
+                in_=grouped[t][:, ci * BANK_COLS : (ci + 1) * BANK_COLS, :].rearrange("p m t -> p (m t)"),
+            )
+
+        def multiply(t):
+            b, r = divmod(t, BLOCK_BATCHES)
+            a_codes, a_scale_bytes = a_mx[b]
+            w_codes, w_scale_bytes = w_mx[b]
+            if r == 0:
+                acc = ps_acc.tile([P, OUTS], F32)
+                accs[b] = acc
+            for s in range(r * BATCH_PASSES, (r + 1) * BATCH_PASSES):
+                cols = slice(s * P, (s + 1) * P)
+                nc.tensor.matmul_mx(
+                    out=accs[b][:],
+                    lhsT=a_codes[:, cols].bitcast(FP8X4),
+                    lhsT_scale=a_scale_bytes[:, cols],
+                    rhs=w_codes[:, cols].bitcast(FP8X4),
+                    rhs_scale=w_scale_bytes[:, cols],
+                    start=(s == 0),
+                    stop=(s == PASSES - 1),
+                )
+
+        def finish(b):
+            result = work.tile([P, OUTS], F32)
+            nc.vector.tensor_add(out=result[:], in0=accs[b][:], in1=bias_all[:, b * OUTS : (b + 1) * OUTS])
+            nc.sync.dma_start(out=out[b], in_=result[:])
+
+        def live(t):
+            return 0 <= t < BATCHES
+
+        with tc.manual_schedule():
+            for t in range(PREFETCH):
+                load(t)
+            nc.sync.dma_start(out=bias_all[:], in_=b7.rearrange("b j -> (b j)").partition_broadcast(P))
+            for ci in range(BATCH_BANKS):
+                transpose_h(0, ci)
+            transpose_w(0, 0)
+            for t in range(BATCHES + A_LAG + 1):
+                if live(t + PREFETCH):
+                    load(t + PREFETCH)
+                if live(t - A_LAG - 1):
+                    multiply(t - A_LAG - 1)
+                if live(t):
+                    statistics(t)
+                for ci in range(BATCH_BANKS):
+                    if live(t + 1):
+                        transpose_h(t + 1, ci)
+                    for g in range(BANK_PASSES):
+                        if live(t - 1):
+                            activations(t - 1, ci, g)
+                        if live(t) and ci == BATCH_BANKS - 1 and g == 0:
+                            spread(t)
+                    if live(t):
+                        copy_w(t, ci)
+                    t_next, ci_next = divmod(t * BATCH_BANKS + ci + 1, BATCH_BANKS)
+                    if live(t) and live(t_next):
+                        transpose_w(t_next, ci_next)
+                if live(t - 1):
+                    regroup(t - 1)
+                if live(t - A_LAG):
+                    quantise(a_grouped, a_mx, "a", t - A_LAG, 0)
+                if live(t):
+                    gain_times_mean(t)
+                if live(t - A_LAG):
+                    quantise(a_grouped, a_mx, "a", t - A_LAG, 1)
+                if live(t):
+                    inverse_spread(t)
+                if live(t - 1):
+                    quantise(w_grouped, w_mx, "w", t - 1, 0)
+                if live(t):
+                    scale_terms(t)
+                if live(t - 1):
+                    quantise(w_grouped, w_mx, "w", t - 1, 1)
+                if live(t):
+                    shift_term(t)
+                if live(t - A_LAG - 1) and (t - A_LAG - 1) % BLOCK_BATCHES == BLOCK_BATCHES - 1:
+                    finish((t - A_LAG - 1) // BLOCK_BATCHES)

@@ -36,6 +36,7 @@ BLOCK_BATCHES = FEATS // BATCH_K
 BATCHES = BLOCKS * BLOCK_BATCHES
 RUN = 4
 A_LAG = 3
+H_BANKS = 2 * BATCH_BANKS + 1
 PREFETCH = 6
 
 FLOPS = 2 * BLOCKS * ROWS * OUTS * FEATS
@@ -48,8 +49,8 @@ def tile_decoder_pa_k_kernel(tc, h6_pre, g6, be6, W7, b7, out):
         rows_pool = ctx.enter_context(tc.tile_pool(name="rows_pool", bufs=PREFETCH + 2))
         block_pool = ctx.enter_context(tc.tile_pool(name="block_pool", bufs=2))
         work = ctx.enter_context(tc.tile_pool(name="work", bufs=3))
-        ps_h = ctx.enter_context(tc.psum_pool(name="ps_h", bufs=3 * BATCH_BANKS))
-        ps_w = ctx.enter_context(tc.psum_pool(name="ps_w", bufs=1))
+        ps_h = ctx.enter_context(tc.psum_pool(name="ps_h", bufs=H_BANKS))
+        ps_w = ctx.enter_context(tc.psum_pool(name="ps_w", bufs=2))
         ps_acc = ctx.enter_context(tc.psum_pool(name="ps_acc", bufs=1))
 
         ident = const.tile([P, P], F32)
@@ -69,21 +70,28 @@ def tile_decoder_pa_k_kernel(tc, h6_pre, g6, be6, W7, b7, out):
                         bank[:, quarter * P : (quarter + 1) * P], words[:, first + u : first + GROUP_K : PAIR], ident[:]
                     )
 
-        affine_ps = ps_h.tile([P, BANK_GROUPS * P], F32, tag="h_ps")
-        for v, vec in enumerate((g6, be6)):
-            vec_rows = const.tile([P, K_PASS], BF16, name="vec_rows%d" % v)
-            nc.scalar.dma_start(out=vec_rows[:], in_=vec.rearrange("b (s w) -> (b s) w", w=K_PASS))
-            for u in range(PAIR):
-                quarter = PAIR * v + u
-                nc.tensor.transpose(
-                    affine_ps[:, quarter * P : (quarter + 1) * P], vec_rows[:].bitcast(F32)[:, u::PAIR], ident[:]
-                )
         affine = const.tile([P, 2, BATCHES * BATCH_FEATS], F32)
-        for v in range(2):
-            nc.vector.tensor_copy(
-                out=affine[:, v, :].rearrange("p (s u e) -> p s u e", u=PAIR, e=PAIR),
-                in_=affine_ps[:].bitcast(BF16).rearrange("p (v u s e) -> p v s u e", v=2, u=PAIR, e=PAIR)[:, v],
-            )
+        vec_rows = []
+
+        def load_affine():
+            for v, vec in enumerate((g6, be6)):
+                rows_tile = const.tile([P, K_PASS], BF16, name="vec_rows%d" % v)
+                nc.sync.dma_start(out=rows_tile[:], in_=vec.rearrange("b (s w) -> (b s) w", w=K_PASS))
+                vec_rows.append(rows_tile)
+
+        def transpose_affine():
+            affine_ps = ps_w.tile([P, BANK_GROUPS * P], F32, tag="w_ps")
+            for v in range(2):
+                for u in range(PAIR):
+                    quarter = PAIR * v + u
+                    nc.tensor.transpose(
+                        affine_ps[:, quarter * P : (quarter + 1) * P], vec_rows[v][:].bitcast(F32)[:, u::PAIR], ident[:]
+                    )
+            for v in range(2):
+                nc.scalar.copy(
+                    out=affine[:, v, :].rearrange("p (s u e) -> p s u e", u=PAIR, e=PAIR),
+                    in_=affine_ps[:].bitcast(BF16).rearrange("p (v u s e) -> p v s u e", v=2, u=PAIR, e=PAIR)[:, v],
+                )
 
         bias_all = const.tile([P, BLOCKS * OUTS], BF16)
 
@@ -92,8 +100,6 @@ def tile_decoder_pa_k_kernel(tc, h6_pre, g6, be6, W7, b7, out):
         h_banks = {}
         w_banks = {}
         stats = {}
-        stds = {}
-        gain_means = {}
         rstds = {}
         means_scaled = {}
         scales = {}
@@ -112,9 +118,12 @@ def tile_decoder_pa_k_kernel(tc, h6_pre, g6, be6, W7, b7, out):
             b, r = divmod(t, BLOCK_BATCHES)
             feats = slice(r * BATCH_K, (r + 1) * BATCH_K)
             h_tile = rows_pool.tile([P, BATCH_K], BF16)
-            nc.sync.dma_start(out=h_tile[:], in_=h6_pre[b][:, feats])
             w_tile = rows_pool.tile([P, BATCH_K], BF16)
-            nc.sync.dma_start(out=w_tile[:], in_=W7[b][:, feats])
+            parts = BATCH_BANKS if t == 0 else 1
+            for rows_tile, source in ((h_tile, h6_pre), (w_tile, W7)):
+                for part in range(parts):
+                    cols = slice(part * BATCH_K // parts, (part + 1) * BATCH_K // parts)
+                    nc.sync.dma_start(out=rows_tile[:, cols], in_=source[b][:, feats][:, cols])
             h_rows[t] = h_tile
             w_rows[t] = w_tile
 
@@ -136,26 +145,24 @@ def tile_decoder_pa_k_kernel(tc, h6_pre, g6, be6, W7, b7, out):
             stats[t] = batch_stats[:].rearrange("p i (e s) -> p s (i e)", s=3)
 
         def spread(t):
-            std = work.tile([P, BATCH_FEATS], F32)
-            nc.scalar.activation(out=std[:], in_=stats[t][:, 2, :], func=ACT.Sqrt, scale=1.0 / ROWS, bias=eps_col[:])
-            stds[t] = std
-
-        def gain_times_mean(t):
-            gain_mean = work.tile([P, BATCH_FEATS], F32)
-            nc.vector.tensor_mul(out=gain_mean[:], in0=stats[t][:, 1, :], in1=affine[:, 0, batch_feats(t)])
-            gain_means[t] = gain_mean
-
-        def inverse_spread(t):
             rstd = work.tile([P, BATCH_FEATS], F32)
-            nc.vector.reciprocal(out=rstd[:], in_=stds[t][:])
+            nc.scalar.activation(
+                out=rstd[:],
+                in_=stats[t][:, 2, :],
+                func=ACT.Abs_reciprocal_sqrt,
+                scale=1.0 / ROWS,
+                bias=eps_col[:],
+            )
             rstds[t] = rstd
 
-        def scale_terms(t):
+        def scale_term(t):
             scale = work.tile([P, BATCH_FEATS], F32)
             nc.vector.tensor_mul(out=scale[:], in0=rstds[t][:], in1=affine[:, 0, batch_feats(t)])
-            mean_scaled = work.tile([P, BATCH_FEATS], F32)
-            nc.vector.tensor_mul(out=mean_scaled[:], in0=rstds[t][:], in1=gain_means[t][:])
             scales[t] = scale
+
+        def scaled_mean(t):
+            mean_scaled = work.tile([P, BATCH_FEATS], F32)
+            nc.vector.tensor_mul(out=mean_scaled[:], in0=stats[t][:, 1, :], in1=scales[t][:])
             means_scaled[t] = mean_scaled
 
         def shift_term(t):
@@ -252,12 +259,15 @@ def tile_decoder_pa_k_kernel(tc, h6_pre, g6, be6, W7, b7, out):
             return 0 <= t < BATCHES
 
         with tc.manual_schedule():
-            for t in range(PREFETCH):
+            load(0)
+            load_affine()
+            for t in range(1, PREFETCH):
                 load(t)
             nc.sync.dma_start(out=bias_all[:], in_=b7.rearrange("b j -> (b j)").partition_broadcast(P))
             for ci in range(BATCH_BANKS):
                 transpose_h(0, ci)
             transpose_w(0, 0)
+            transpose_affine()
             for t in range(BATCHES + A_LAG + 1):
                 if live(t + PREFETCH):
                     load(t + PREFETCH)
@@ -282,16 +292,13 @@ def tile_decoder_pa_k_kernel(tc, h6_pre, g6, be6, W7, b7, out):
                     regroup(t - 1)
                 if live(t - A_LAG):
                     quantise(a_grouped, a_mx, "a", t - A_LAG, 0)
-                if live(t):
-                    gain_times_mean(t)
-                if live(t - A_LAG):
                     quantise(a_grouped, a_mx, "a", t - A_LAG, 1)
                 if live(t):
-                    inverse_spread(t)
+                    scale_term(t)
                 if live(t - 1):
                     quantise(w_grouped, w_mx, "w", t - 1, 0)
                 if live(t):
-                    scale_terms(t)
+                    scaled_mean(t)
                 if live(t - 1):
                     quantise(w_grouped, w_mx, "w", t - 1, 1)
                 if live(t):

@@ -59,6 +59,8 @@ def tile_decoder_pa_k_kernel(tc, h6_pre, g6, be6, W7, b7, out):
         nc.vector.memset(zero_col[:], 0.0)
         eps_col = const.tile([P, 1], F32)
         nc.vector.tensor_scalar(out=eps_col[:], in0=zero_col[:], scalar1=1.0, scalar2=EPS, op0=ALU.mult, op1=ALU.add)
+        warm_col = const.tile([P, 1], F32)
+        nc.scalar.activation(out=warm_col[:], in_=zero_col[:], func=ACT.Abs_reciprocal_sqrt, bias=eps_col[:])
 
         def transpose_bank(bank, rows_tile, ci):
             words = rows_tile[:].bitcast(F32)
@@ -170,7 +172,7 @@ def tile_decoder_pa_k_kernel(tc, h6_pre, g6, be6, W7, b7, out):
             nc.vector.tensor_sub(out=shift[:], in0=affine[:, 1, batch_feats(t)], in1=means_scaled[t][:])
             shifts[t] = shift
 
-        def activations(t, ci, g):
+        def activations(on_vector, t, ci, g):
             if ci == 0 and g == 0:
                 planes_tile = work.tile([P, PACK, BATCH_COLS], BF16)
                 a_planes[t] = planes_tile
@@ -181,16 +183,19 @@ def tile_decoder_pa_k_kernel(tc, h6_pre, g6, be6, W7, b7, out):
             for u in range(PAIR):
                 for e in range(PAIR):
                     col = PAIR * (BANK_GROUPS * ci + PAIR * g + u) + e
-                    nc.scalar.activation(
-                        out=a_planes[t][:, PAIR * u + e, first : first + ROWS],
-                        in_=halves[:, u, g, :, e],
-                        func=ACT.Relu,
-                        scale=scales[t][:, col : col + 1],
-                        bias=shifts[t][:, col : col + 1],
-                    )
+                    plane = a_planes[t][:, PAIR * u + e, first : first + ROWS]
+                    scale = scales[t][:, col : col + 1]
+                    shift = shifts[t][:, col : col + 1]
+                    if on_vector:
+                        nc.vector.tensor_scalar(
+                            out=plane, in0=halves[:, u, g, :, e], scalar1=scale, scalar2=shift, op0=ALU.mult, op1=ALU.add
+                        )
+                    else:
+                        nc.scalar.activation(out=plane, in_=halves[:, u, g, :, e], func=ACT.Relu, scale=scale, bias=shift)
 
         def regroup(t):
             grouped_tile = work.tile([P, BATCH_COLS, PACK], BF16, name="a_grouped", align_bytes=64)
+            a_grouped[t] = grouped_tile
             nc.gpsimd.tensor_scalar(
                 out=grouped_tile[:].rearrange("p (c i) t -> p c t i", i=RUN),
                 in0=a_planes[t][:].rearrange("p t (c i) -> p c t i", i=RUN),
@@ -199,7 +204,20 @@ def tile_decoder_pa_k_kernel(tc, h6_pre, g6, be6, W7, b7, out):
                 op0=ALU.mult,
                 op1=ALU.add,
             )
-            a_grouped[t] = grouped_tile
+
+        def regroup_last(t, ci):
+            if ci == 0:
+                grouped_tile = work.tile([P, BATCH_COLS, PACK], BF16, name="a_grouped", align_bytes=64)
+                a_grouped[t] = grouped_tile
+            cols = slice(ci * BANK_COLS, (ci + 1) * BANK_COLS)
+            nc.vector.tensor_scalar(
+                out=a_grouped[t][:, cols, :].rearrange("p (c i) t -> p c t i", i=RUN),
+                in0=a_planes[t][:, :, cols].rearrange("p t (c i) -> p c t i", i=RUN),
+                scalar1=1.0,
+                scalar2=0.0,
+                op0=ALU.mult,
+                op1=ALU.max,
+            )
 
         def transpose_w(t, ci):
             w_ps = ps_w.tile([P, BANK_GROUPS * P], F32)
@@ -280,7 +298,8 @@ def tile_decoder_pa_k_kernel(tc, h6_pre, g6, be6, W7, b7, out):
                         transpose_h(t + 1, ci)
                     for g in range(BANK_PASSES):
                         if live(t - 1):
-                            activations(t - 1, ci, g)
+                            on_vector = t == BATCHES and ci == BATCH_BANKS - 1
+                            activations(on_vector, t - 1, ci, g)
                         if live(t) and ci == BATCH_BANKS - 1 and g == 0:
                             spread(t)
                     if live(t):
@@ -288,11 +307,13 @@ def tile_decoder_pa_k_kernel(tc, h6_pre, g6, be6, W7, b7, out):
                     t_next, ci_next = divmod(t * BATCH_BANKS + ci + 1, BATCH_BANKS)
                     if live(t) and live(t_next):
                         transpose_w(t_next, ci_next)
-                if live(t - 1):
+                if live(t - 1) and t < BATCHES:
                     regroup(t - 1)
-                if live(t - A_LAG):
-                    quantise(a_grouped, a_mx, "a", t - A_LAG, 0)
-                    quantise(a_grouped, a_mx, "a", t - A_LAG, 1)
+                for ci in range(BATCH_BANKS):
+                    if t - A_LAG == BATCHES - 1:
+                        regroup_last(t - A_LAG, ci)
+                    if live(t - A_LAG):
+                        quantise(a_grouped, a_mx, "a", t - A_LAG, ci)
                 if live(t):
                     scale_term(t)
                 if live(t - 1):

@@ -36,7 +36,9 @@ BLOCK_BATCHES = FEATS // BATCH_K
 BATCHES = BLOCKS * BLOCK_BATCHES
 RUN = 4
 A_LAG = 3
+GPSIMD_COLS = 464
 H_BANKS = 2 * BATCH_BANKS + 1
+VECTOR_BATCHES = 2
 PREFETCH = 6
 
 FLOPS = 2 * BLOCKS * ROWS * OUTS * FEATS
@@ -46,7 +48,7 @@ def tile_decoder_pa_k_kernel(tc, h6_pre, g6, be6, W7, b7, out):
     nc = tc.nc
     with ExitStack() as ctx:
         const = ctx.enter_context(tc.tile_pool(name="const", bufs=1))
-        rows_pool = ctx.enter_context(tc.tile_pool(name="rows_pool", bufs=PREFETCH + 2))
+        rows_pool = ctx.enter_context(tc.tile_pool(name="rows_pool", bufs=2 * PREFETCH + 5))
         block_pool = ctx.enter_context(tc.tile_pool(name="block_pool", bufs=2))
         work = ctx.enter_context(tc.tile_pool(name="work", bufs=3))
         ps_h = ctx.enter_context(tc.psum_pool(name="ps_h", bufs=H_BANKS))
@@ -116,18 +118,13 @@ def tile_decoder_pa_k_kernel(tc, h6_pre, g6, be6, W7, b7, out):
         def batch_feats(t):
             return slice(t * BATCH_FEATS, (t + 1) * BATCH_FEATS)
 
-        def load(t):
+        def load(rows, source, t, part=0, parts=1):
+            if part == 0:
+                rows_tile = rows_pool.tile([P, BATCH_K], BF16)
+                rows[t] = rows_tile
             b, r = divmod(t, BLOCK_BATCHES)
-            feats = slice(r * BATCH_K, (r + 1) * BATCH_K)
-            h_tile = rows_pool.tile([P, BATCH_K], BF16)
-            w_tile = rows_pool.tile([P, BATCH_K], BF16)
-            parts = BATCH_BANKS if t == 0 else 1
-            for rows_tile, source in ((h_tile, h6_pre), (w_tile, W7)):
-                for part in range(parts):
-                    cols = slice(part * BATCH_K // parts, (part + 1) * BATCH_K // parts)
-                    nc.sync.dma_start(out=rows_tile[:, cols], in_=source[b][:, feats][:, cols])
-            h_rows[t] = h_tile
-            w_rows[t] = w_tile
+            first, last = (part * BATCH_K // parts, (part + 1) * BATCH_K // parts)
+            nc.sync.dma_start(out=rows[t][:, first:last], in_=source[b][:, r * BATCH_K + first : r * BATCH_K + last])
 
         def transpose_h(t, ci):
             h_ps = ps_h.tile([P, BANK_GROUPS * P], F32)
@@ -172,7 +169,7 @@ def tile_decoder_pa_k_kernel(tc, h6_pre, g6, be6, W7, b7, out):
             nc.vector.tensor_sub(out=shift[:], in0=affine[:, 1, batch_feats(t)], in1=means_scaled[t][:])
             shifts[t] = shift
 
-        def activations(on_vector, t, ci, g):
+        def activations(t, ci, g):
             if ci == 0 and g == 0:
                 planes_tile = work.tile([P, PACK, BATCH_COLS], BF16)
                 a_planes[t] = planes_tile
@@ -183,41 +180,34 @@ def tile_decoder_pa_k_kernel(tc, h6_pre, g6, be6, W7, b7, out):
             for u in range(PAIR):
                 for e in range(PAIR):
                     col = PAIR * (BANK_GROUPS * ci + PAIR * g + u) + e
-                    plane = a_planes[t][:, PAIR * u + e, first : first + ROWS]
-                    scale = scales[t][:, col : col + 1]
-                    shift = shifts[t][:, col : col + 1]
-                    if on_vector:
-                        nc.vector.tensor_scalar(
-                            out=plane, in0=halves[:, u, g, :, e], scalar1=scale, scalar2=shift, op0=ALU.mult, op1=ALU.add
-                        )
-                    else:
-                        nc.scalar.activation(out=plane, in_=halves[:, u, g, :, e], func=ACT.Relu, scale=scale, bias=shift)
+                    nc.scalar.activation(
+                        out=a_planes[t][:, PAIR * u + e, first : first + ROWS],
+                        in_=halves[:, u, g, :, e],
+                        func=ACT.Relu,
+                        scale=scales[t][:, col : col + 1],
+                        bias=shifts[t][:, col : col + 1],
+                    )
 
-        def regroup(t):
-            grouped_tile = work.tile([P, BATCH_COLS, PACK], BF16, name="a_grouped", align_bytes=64)
-            a_grouped[t] = grouped_tile
-            nc.gpsimd.tensor_scalar(
-                out=grouped_tile[:].rearrange("p (c i) t -> p c t i", i=RUN),
-                in0=a_planes[t][:].rearrange("p t (c i) -> p c t i", i=RUN),
-                scalar1=1.0,
-                scalar2=0.0,
-                op0=ALU.mult,
-                op1=ALU.add,
-            )
-
-        def regroup_last(t, ci):
-            if ci == 0:
+        def regroup_views(t, first, last):
+            if t not in a_grouped:
                 grouped_tile = work.tile([P, BATCH_COLS, PACK], BF16, name="a_grouped", align_bytes=64)
                 a_grouped[t] = grouped_tile
-            cols = slice(ci * BANK_COLS, (ci + 1) * BANK_COLS)
-            nc.vector.tensor_scalar(
-                out=a_grouped[t][:, cols, :].rearrange("p (c i) t -> p c t i", i=RUN),
-                in0=a_planes[t][:, :, cols].rearrange("p t (c i) -> p c t i", i=RUN),
-                scalar1=1.0,
-                scalar2=0.0,
-                op0=ALU.mult,
-                op1=ALU.max,
+            return (
+                a_grouped[t][:, first:last, :].rearrange("p (c i) t -> p c t i", i=RUN),
+                a_planes[t][:, :, first:last].rearrange("p t (c i) -> p c t i", i=RUN),
             )
+
+        def regroup(t):
+            grouped, planes = regroup_views(t, 0, GPSIMD_COLS)
+            nc.gpsimd.tensor_scalar(out=grouped, in0=planes, scalar1=1.0, scalar2=0.0, op0=ALU.mult, op1=ALU.add)
+
+        def regroup_rest(t):
+            grouped, planes = regroup_views(t, GPSIMD_COLS, BATCH_COLS)
+            nc.scalar.copy(out=grouped, in_=planes)
+
+        def regroup_last(t, ci):
+            grouped, planes = regroup_views(t, ci * BANK_COLS, (ci + 1) * BANK_COLS)
+            nc.vector.tensor_copy(out=grouped, in_=planes)
 
         def transpose_w(t, ci):
             w_ps = ps_w.tile([P, BANK_GROUPS * P], F32)
@@ -277,18 +267,25 @@ def tile_decoder_pa_k_kernel(tc, h6_pre, g6, be6, W7, b7, out):
             return 0 <= t < BATCHES
 
         with tc.manual_schedule():
-            load(0)
+            load(h_rows, h6_pre, 0, 0, BATCH_BANKS)
             load_affine()
+            load(h_rows, h6_pre, 0, 1, BATCH_BANKS)
+            load(w_rows, W7, 0, 0, BATCH_BANKS)
+            load(h_rows, h6_pre, 1)
+            load(w_rows, W7, 0, 1, BATCH_BANKS)
             for t in range(1, PREFETCH):
-                load(t)
+                load(h_rows, h6_pre, t + 1)
+                load(w_rows, W7, t)
             nc.sync.dma_start(out=bias_all[:], in_=b7.rearrange("b j -> (b j)").partition_broadcast(P))
-            for ci in range(BATCH_BANKS):
-                transpose_h(0, ci)
-            transpose_w(0, 0)
+            transpose_h(0, 0)
             transpose_affine()
+            transpose_h(0, 1)
+            transpose_w(0, 0)
             for t in range(BATCHES + A_LAG + 1):
+                if live(t + PREFETCH + 1):
+                    load(h_rows, h6_pre, t + PREFETCH + 1)
                 if live(t + PREFETCH):
-                    load(t + PREFETCH)
+                    load(w_rows, W7, t + PREFETCH)
                 if live(t - A_LAG - 1):
                     multiply(t - A_LAG - 1)
                 if live(t):
@@ -298,22 +295,22 @@ def tile_decoder_pa_k_kernel(tc, h6_pre, g6, be6, W7, b7, out):
                         transpose_h(t + 1, ci)
                     for g in range(BANK_PASSES):
                         if live(t - 1):
-                            on_vector = t == BATCHES and ci == BATCH_BANKS - 1
-                            activations(on_vector, t - 1, ci, g)
-                        if live(t) and ci == BATCH_BANKS - 1 and g == 0:
+                            activations(t - 1, ci, g)
+                        if live(t) and (ci, g) == (0 if t == 0 else BATCH_BANKS - 1, 0):
                             spread(t)
-                    if live(t):
-                        copy_w(t, ci)
-                    t_next, ci_next = divmod(t * BATCH_BANKS + ci + 1, BATCH_BANKS)
-                    if live(t) and live(t_next):
-                        transpose_w(t_next, ci_next)
-                if live(t - 1) and t < BATCHES:
+                    w_bank = t * BATCH_BANKS + ci - 1
+                    if 0 <= w_bank < BATCHES * BATCH_BANKS:
+                        copy_w(*divmod(w_bank, BATCH_BANKS))
+                    if 0 <= w_bank < BATCHES * BATCH_BANKS - 1:
+                        transpose_w(*divmod(w_bank + 1, BATCH_BANKS))
+                if live(t - 1) and t - 1 < BATCHES - VECTOR_BATCHES:
                     regroup(t - 1)
+                    regroup_rest(t - 1)
                 for ci in range(BATCH_BANKS):
-                    if t - A_LAG == BATCHES - 1:
-                        regroup_last(t - A_LAG, ci)
                     if live(t - A_LAG):
                         quantise(a_grouped, a_mx, "a", t - A_LAG, ci)
+                    if live(t - A_LAG + 1) and t - A_LAG + 1 >= BATCHES - VECTOR_BATCHES:
+                        regroup_last(t - A_LAG + 1, ci)
                 if live(t):
                     scale_term(t)
                 if live(t - 1):

@@ -36,7 +36,7 @@ BLOCK_BATCHES = FEATS // BATCH_K
 BATCHES = BLOCKS * BLOCK_BATCHES
 RUN = 4
 A_LAG = 3
-GPSIMD_COLS = 464
+GPSIMD_COLS = 448
 H_BANKS = 2 * BATCH_BANKS + 1
 VECTOR_BATCHES = 2
 PREFETCH = 6
@@ -201,12 +201,8 @@ def tile_decoder_pa_k_kernel(tc, h6_pre, g6, be6, W7, b7, out):
             grouped, planes = regroup_views(t, 0, GPSIMD_COLS)
             nc.gpsimd.tensor_scalar(out=grouped, in0=planes, scalar1=1.0, scalar2=0.0, op0=ALU.mult, op1=ALU.add)
 
-        def regroup_rest(t):
-            grouped, planes = regroup_views(t, GPSIMD_COLS, BATCH_COLS)
-            nc.scalar.copy(out=grouped, in_=planes)
-
-        def regroup_last(t, ci):
-            grouped, planes = regroup_views(t, ci * BANK_COLS, (ci + 1) * BANK_COLS)
+        def regroup_on_vector(t, first, last):
+            grouped, planes = regroup_views(t, first, last)
             nc.vector.tensor_copy(out=grouped, in_=planes)
 
         def transpose_w(t, ci):
@@ -305,18 +301,19 @@ def tile_decoder_pa_k_kernel(tc, h6_pre, g6, be6, W7, b7, out):
                         transpose_w(*divmod(w_bank + 1, BATCH_BANKS))
                 if live(t - 1) and t - 1 < BATCHES - VECTOR_BATCHES:
                     regroup(t - 1)
-                    regroup_rest(t - 1)
                 for ci in range(BATCH_BANKS):
                     if live(t - A_LAG):
                         quantise(a_grouped, a_mx, "a", t - A_LAG, ci)
                     if live(t - A_LAG + 1) and t - A_LAG + 1 >= BATCHES - VECTOR_BATCHES:
-                        regroup_last(t - A_LAG + 1, ci)
+                        regroup_on_vector(t - A_LAG + 1, ci * BANK_COLS, (ci + 1) * BANK_COLS)
                 if live(t):
                     scale_term(t)
                 if live(t - 1):
                     quantise(w_grouped, w_mx, "w", t - 1, 0)
                 if live(t):
                     scaled_mean(t)
+                if live(t - 2) and t - 2 < BATCHES - VECTOR_BATCHES:
+                    regroup_on_vector(t - 2, GPSIMD_COLS, BATCH_COLS)
                 if live(t - 1):
                     quantise(w_grouped, w_mx, "w", t - 1, 1)
                 if live(t):

@@ -173,6 +173,8 @@ def tile_decoder_pa_k_kernel(tc, h6_pre, g6, be6, W7, b7, out):
             if ci == 0 and g == 0:
                 planes_tile = work.tile([P, PACK, BATCH_COLS], BF16)
                 a_planes[t] = planes_tile
+                grouped_tile = work.tile([P, BATCH_COLS, PACK], BF16, name="a_grouped", align_bytes=64)
+                a_grouped[t] = grouped_tile
             halves = h_banks[t, ci][:].bitcast(BF16).rearrange(
                 "p (u g n e) -> p u g n e", u=PAIR, g=BANK_PASSES, e=PAIR
             )
@@ -188,22 +190,20 @@ def tile_decoder_pa_k_kernel(tc, h6_pre, g6, be6, W7, b7, out):
                         bias=shifts[t][:, col : col + 1],
                     )
 
-        def regroup_views(t, first, last):
-            if t not in a_grouped:
-                grouped_tile = work.tile([P, BATCH_COLS, PACK], BF16, name="a_grouped", align_bytes=64)
-                a_grouped[t] = grouped_tile
-            return (
-                a_grouped[t][:, first:last, :].rearrange("p (c i) t -> p c t i", i=RUN),
-                a_planes[t][:, :, first:last].rearrange("p t (c i) -> p c t i", i=RUN),
+        def regroup(t):
+            nc.gpsimd.tensor_scalar(
+                out=a_grouped[t][:, :GPSIMD_COLS, :].rearrange("p (c i) t -> p c t i", i=RUN),
+                in0=a_planes[t][:, :, :GPSIMD_COLS].rearrange("p t (c i) -> p c t i", i=RUN),
+                scalar1=1.0,
+                scalar2=0.0,
+                op0=ALU.mult,
+                op1=ALU.add,
             )
 
-        def regroup(t):
-            grouped, planes = regroup_views(t, 0, GPSIMD_COLS)
-            nc.gpsimd.tensor_scalar(out=grouped, in0=planes, scalar1=1.0, scalar2=0.0, op0=ALU.mult, op1=ALU.add)
-
         def regroup_on_vector(t, first, last):
-            grouped, planes = regroup_views(t, first, last)
-            nc.vector.tensor_copy(out=grouped, in_=planes)
+            nc.vector.tensor_copy(
+                out=a_grouped[t][:, first:last, :], in_=a_planes[t][:, :, first:last].rearrange("p t c -> p c t")
+            )
 
         def transpose_w(t, ci):
             w_ps = ps_w.tile([P, BANK_GROUPS * P], F32)
@@ -220,7 +220,7 @@ def tile_decoder_pa_k_kernel(tc, h6_pre, g6, be6, W7, b7, out):
                 in_=w_banks[t, ci][:].rearrange("p (u m) -> p m u", u=PAIR),
             )
 
-        def quantise(grouped, mx, name, t, ci):
+        def quantise(grouped, mx, name, t, ci, banks=1):
             b, r = divmod(t, BLOCK_BATCHES)
             if r == 0 and ci == 0:
                 codes_tile = block_pool.tile([P, PASSES * P], U32, name=name + "_codes", align_bytes=64)
@@ -228,11 +228,11 @@ def tile_decoder_pa_k_kernel(tc, h6_pre, g6, be6, W7, b7, out):
                 mx[b] = (codes_tile, scale_bytes)
             codes_tile, scale_bytes = mx[b]
             first = r * BATCH_COLS + ci * BANK_COLS
-            cols = slice(first, first + BANK_COLS)
+            cols = slice(first, first + banks * BANK_COLS)
             nc.vector.quantize_mx(
                 out=codes_tile[:, cols].bitcast(FP8X4),
                 scales=scale_bytes[:, cols],
-                in_=grouped[t][:, ci * BANK_COLS : (ci + 1) * BANK_COLS, :].rearrange("p m t -> p (m t)"),
+                in_=grouped[t][:, ci * BANK_COLS : (ci + banks) * BANK_COLS, :].rearrange("p m t -> p (m t)"),
             )
 
         def multiply(t):
@@ -302,7 +302,9 @@ def tile_decoder_pa_k_kernel(tc, h6_pre, g6, be6, W7, b7, out):
                 if live(t - 1) and t - 1 < BATCHES - VECTOR_BATCHES:
                     regroup(t - 1)
                 for ci in range(BATCH_BANKS):
-                    if live(t - A_LAG):
+                    if live(t - A_LAG) and t - A_LAG < BATCHES - VECTOR_BATCHES and ci == 0:
+                        quantise(a_grouped, a_mx, "a", t - A_LAG, 0, BATCH_BANKS)
+                    if live(t - A_LAG) and t - A_LAG >= BATCHES - VECTOR_BATCHES:
                         quantise(a_grouped, a_mx, "a", t - A_LAG, ci)
                     if live(t - A_LAG + 1) and t - A_LAG + 1 >= BATCHES - VECTOR_BATCHES:
                         regroup_on_vector(t - A_LAG + 1, ci * BANK_COLS, (ci + 1) * BANK_COLS)

@@ -22,24 +22,22 @@ PACK = 4
 PAIR = 2
 GROUP_K = P * PAIR
 K_PASS = P * PACK
-PASSES = FEATS // K_PASS
 BANK_GROUPS = 4
 BANK_PASSES = 2
+BANK_K = BANK_GROUPS * GROUP_K
+BANK_FEATS = BANK_GROUPS * PAIR
 BANK_COLS = BANK_PASSES * ROWS
+BLOCK_BANKS = FEATS // BANK_K
+BANKS = BLOCKS * BLOCK_BANKS
+H_BANKS = 5
 BATCH_BANKS = 2
-BATCH_K = BATCH_BANKS * BANK_GROUPS * GROUP_K
-BATCH_GROUPS = BATCH_BANKS * BANK_GROUPS
-BATCH_FEATS = BATCH_GROUPS * PAIR
-BATCH_PASSES = BATCH_BANKS * BANK_PASSES
-BATCH_COLS = BATCH_BANKS * BANK_COLS
-BLOCK_BATCHES = FEATS // BATCH_K
-BATCHES = BLOCKS * BLOCK_BATCHES
-RUN = 4
-A_LAG = 3
-GPSIMD_COLS = 448
-H_BANKS = 2 * BATCH_BANKS + 1
-VECTOR_BATCHES = 2
+BATCHES = BANKS // BATCH_BANKS
+BATCH_FEATS = BATCH_BANKS * BANK_FEATS
 PREFETCH = 6
+BEHIND = 1
+RUN = 4
+GPSIMD_COLS = 464
+VECTOR_ROUNDS = 3
 
 FLOPS = 2 * BLOCKS * ROWS * OUTS * FEATS
 
@@ -50,7 +48,7 @@ def tile_decoder_pa_k_kernel(tc, h6_pre, g6, be6, W7, b7, out):
         const = ctx.enter_context(tc.tile_pool(name="const", bufs=1))
         rows_pool = ctx.enter_context(tc.tile_pool(name="rows_pool", bufs=2 * PREFETCH + 5))
         block_pool = ctx.enter_context(tc.tile_pool(name="block_pool", bufs=2))
-        work = ctx.enter_context(tc.tile_pool(name="work", bufs=3))
+        work = ctx.enter_context(tc.tile_pool(name="work", bufs=4))
         ps_h = ctx.enter_context(tc.psum_pool(name="ps_h", bufs=H_BANKS))
         ps_w = ctx.enter_context(tc.psum_pool(name="ps_w", bufs=2))
         ps_acc = ctx.enter_context(tc.psum_pool(name="ps_acc", bufs=1))
@@ -64,18 +62,48 @@ def tile_decoder_pa_k_kernel(tc, h6_pre, g6, be6, W7, b7, out):
         warm_col = const.tile([P, 1], F32)
         nc.scalar.activation(out=warm_col[:], in_=zero_col[:], func=ACT.Abs_reciprocal_sqrt, bias=eps_col[:])
 
-        def transpose_bank(bank, rows_tile, ci):
-            words = rows_tile[:].bitcast(F32)
+        bias_all = const.tile([P, BLOCKS * OUTS], BF16)
+        affine = const.tile([P, 2, BANKS * BANK_FEATS], F32)
+        vec_rows = []
+
+        h_rows = {}
+        w_rows = {}
+        h_banks = {}
+        w_banks = {}
+        stats_tiles = {}
+        stats = {}
+        rstds = {}
+        means_scaled = {}
+        scales = {}
+        shifts = {}
+        a_planes = {}
+        a_grouped = {}
+        w_grouped = {}
+        a_mx = {}
+        w_mx = {}
+        accs = {}
+
+        def load(rows, source, i, part=0, parts=1):
+            if part == 0:
+                rows_tile = rows_pool.tile([P, BATCH_BANKS * BANK_K], BF16)
+                rows[i] = rows_tile
+            b, r = divmod(i * BATCH_BANKS, BLOCK_BANKS)
+            first, last = (part * BATCH_BANKS * BANK_K // parts, (part + 1) * BATCH_BANKS * BANK_K // parts)
+            nc.sync.dma_start(
+                out=rows[i][:, first:last], in_=source[b][:, r * BANK_K + first : r * BANK_K + last]
+            )
+
+        def transpose_bank(bank, rows, q):
+            i, part = divmod(q, BATCH_BANKS)
+            words = rows[i][:, part * BANK_K : (part + 1) * BANK_K].bitcast(F32)
             for g in range(BANK_PASSES):
                 for u in range(PAIR):
-                    first = (BANK_PASSES * ci + g) * GROUP_K
                     quarter = BANK_PASSES * u + g
                     nc.tensor.transpose(
-                        bank[:, quarter * P : (quarter + 1) * P], words[:, first + u : first + GROUP_K : PAIR], ident[:]
+                        bank[:, quarter * P : (quarter + 1) * P],
+                        words[:, g * GROUP_K + u : (g + 1) * GROUP_K : PAIR],
+                        ident[:],
                     )
-
-        affine = const.tile([P, 2, BATCHES * BATCH_FEATS], F32)
-        vec_rows = []
 
         def load_affine():
             for v, vec in enumerate((g6, be6)):
@@ -97,49 +125,25 @@ def tile_decoder_pa_k_kernel(tc, h6_pre, g6, be6, W7, b7, out):
                     in_=affine_ps[:].bitcast(BF16).rearrange("p (v u s e) -> p v s u e", v=2, u=PAIR, e=PAIR)[:, v],
                 )
 
-        bias_all = const.tile([P, BLOCKS * OUTS], BF16)
-
-        h_rows = {}
-        w_rows = {}
-        h_banks = {}
-        w_banks = {}
-        stats = {}
-        rstds = {}
-        means_scaled = {}
-        scales = {}
-        shifts = {}
-        a_planes = {}
-        a_grouped = {}
-        w_grouped = {}
-        a_mx = {}
-        w_mx = {}
-        accs = {}
-
-        def batch_feats(t):
-            return slice(t * BATCH_FEATS, (t + 1) * BATCH_FEATS)
-
-        def load(rows, source, t, part=0, parts=1):
-            if part == 0:
-                rows_tile = rows_pool.tile([P, BATCH_K], BF16)
-                rows[t] = rows_tile
-            b, r = divmod(t, BLOCK_BATCHES)
-            first, last = (part * BATCH_K // parts, (part + 1) * BATCH_K // parts)
-            nc.sync.dma_start(out=rows[t][:, first:last], in_=source[b][:, r * BATCH_K + first : r * BATCH_K + last])
-
-        def transpose_h(t, ci):
+        def transpose_h(q):
             h_ps = ps_h.tile([P, BANK_GROUPS * P], F32)
-            transpose_bank(h_ps, h_rows[t], ci)
-            h_banks[t, ci] = h_ps
+            transpose_bank(h_ps, h_rows, q)
+            h_banks[q] = h_ps
+
+        def transpose_w(q):
+            w_ps = ps_w.tile([P, BANK_GROUPS * P], F32)
+            transpose_bank(w_ps, w_rows, q)
+            w_banks[q] = w_ps
 
         def statistics(t):
-            batch_stats = work.tile([P, BATCH_GROUPS, 6], F32)
-            for ci in range(BATCH_BANKS):
+            batch_stats = work.tile([P, BATCH_BANKS * BANK_GROUPS, 6], F32)
+            for j in range(BATCH_BANKS):
                 for g in range(BANK_PASSES):
                     for u in range(PAIR):
                         quarter = BANK_PASSES * u + g
                         nc.vector.bn_stats(
-                            out=batch_stats[:, BANK_GROUPS * ci + PAIR * g + u, :],
-                            in_=h_banks[t, ci][:, quarter * P : (quarter + 1) * P].bitcast(BF16),
+                            out=batch_stats[:, BANK_GROUPS * j + PAIR * g + u, :],
+                            in_=h_banks[t * BATCH_BANKS + j][:, quarter * P : (quarter + 1) * P].bitcast(BF16),
                         )
             stats[t] = batch_stats[:].rearrange("p i (e s) -> p s (i e)", s=3)
 
@@ -153,6 +157,9 @@ def tile_decoder_pa_k_kernel(tc, h6_pre, g6, be6, W7, b7, out):
                 bias=eps_col[:],
             )
             rstds[t] = rstd
+
+        def batch_feats(t):
+            return slice(t * BATCH_FEATS, (t + 1) * BATCH_FEATS)
 
         def scale_term(t):
             scale = work.tile([P, BATCH_FEATS], F32)
@@ -169,80 +176,95 @@ def tile_decoder_pa_k_kernel(tc, h6_pre, g6, be6, W7, b7, out):
             nc.vector.tensor_sub(out=shift[:], in0=affine[:, 1, batch_feats(t)], in1=means_scaled[t][:])
             shifts[t] = shift
 
-        def activations(t, ci, g):
-            if ci == 0 and g == 0:
-                planes_tile = work.tile([P, PACK, BATCH_COLS], BF16)
-                a_planes[t] = planes_tile
-                grouped_tile = work.tile([P, BATCH_COLS, PACK], BF16, name="a_grouped", align_bytes=64)
-                a_grouped[t] = grouped_tile
-            halves = h_banks[t, ci][:].bitcast(BF16).rearrange(
-                "p (u g n e) -> p u g n e", u=PAIR, g=BANK_PASSES, e=PAIR
-            )
-            first = ci * BANK_COLS + g * ROWS
+        def round_banks(r):
+            first = (r - 1) * BATCH_BANKS - BEHIND
+            return [q for q in range(first, first + BATCH_BANKS) if 0 <= q < BANKS]
+
+        def activations(r, q, g):
+            if q == round_banks(r)[0] and g == 0:
+                planes_tile = work.tile([P, PACK, BATCH_BANKS * BANK_COLS], BF16)
+                a_planes[r] = planes_tile
+                a_grouped_tile = work.tile([P, BATCH_BANKS * BANK_COLS, PACK], BF16, align_bytes=64)
+                a_grouped[r] = a_grouped_tile
+            t, j = divmod(q, BATCH_BANKS)
+            halves = h_banks[q][:].bitcast(BF16).rearrange("p (u g n e) -> p u g n e", u=PAIR, g=BANK_PASSES, e=PAIR)
+            first = round_banks(r).index(q) * BANK_COLS + g * ROWS
             for u in range(PAIR):
                 for e in range(PAIR):
-                    col = PAIR * (BANK_GROUPS * ci + PAIR * g + u) + e
+                    col = BANK_FEATS * j + PACK * g + PAIR * u + e
                     nc.scalar.activation(
-                        out=a_planes[t][:, PAIR * u + e, first : first + ROWS],
+                        out=a_planes[r][:, PAIR * u + e, first : first + ROWS],
                         in_=halves[:, u, g, :, e],
                         func=ACT.Relu,
                         scale=scales[t][:, col : col + 1],
                         bias=shifts[t][:, col : col + 1],
                     )
 
-        def regroup(t):
+        def on_gpsimd(r):
+            return len(round_banks(r)) == BATCH_BANKS and r <= BATCHES + 1 - VECTOR_ROUNDS
+
+        def regroup(r):
             nc.gpsimd.tensor_scalar(
-                out=a_grouped[t][:, :GPSIMD_COLS, :].rearrange("p (c i) t -> p c t i", i=RUN),
-                in0=a_planes[t][:, :, :GPSIMD_COLS].rearrange("p t (c i) -> p c t i", i=RUN),
+                out=a_grouped[r][:, :GPSIMD_COLS, :].rearrange("p (c i) t -> p c t i", i=RUN),
+                in0=a_planes[r][:, :, :GPSIMD_COLS].rearrange("p t (c i) -> p c t i", i=RUN),
                 scalar1=1.0,
                 scalar2=0.0,
                 op0=ALU.mult,
                 op1=ALU.add,
             )
 
-        def regroup_on_vector(t, first, last):
+        def regroup_on_vector(r, first, last):
             nc.vector.tensor_copy(
-                out=a_grouped[t][:, first:last, :], in_=a_planes[t][:, :, first:last].rearrange("p t c -> p c t")
+                out=a_grouped[r][:, first:last, :], in_=a_planes[r][:, :, first:last].rearrange("p t c -> p c t")
             )
 
-        def transpose_w(t, ci):
-            w_ps = ps_w.tile([P, BANK_GROUPS * P], F32)
-            transpose_bank(w_ps, w_rows[t], ci)
-            w_banks[t, ci] = w_ps
-
-        def copy_w(t, ci):
-            if ci == 0:
-                grouped_tile = work.tile([P, BATCH_COLS, PACK], BF16, name="w_grouped", align_bytes=64)
-                w_grouped[t] = grouped_tile
-            part = w_grouped[t][:, ci * BANK_COLS : (ci + 1) * BANK_COLS, :]
+        def copy_w(q):
+            t, j = divmod(q, BATCH_BANKS)
+            if j == 0:
+                w_grouped_tile = work.tile([P, BATCH_BANKS * BANK_COLS, PACK], BF16, align_bytes=64)
+                w_grouped[t] = w_grouped_tile
+            part = w_grouped[t][:, j * BANK_COLS : (j + 1) * BANK_COLS, :]
             nc.scalar.copy(
                 out=part.rearrange("p m t -> p (m t)").bitcast(F32).rearrange("p (m u) -> p m u", u=PAIR),
-                in_=w_banks[t, ci][:].rearrange("p (u m) -> p m u", u=PAIR),
+                in_=w_banks[q][:].rearrange("p (u m) -> p m u", u=PAIR),
             )
 
-        def quantise(grouped, mx, name, t, ci, banks=1):
-            b, r = divmod(t, BLOCK_BATCHES)
-            if r == 0 and ci == 0:
-                codes_tile = block_pool.tile([P, PASSES * P], U32, name=name + "_codes", align_bytes=64)
-                scale_bytes = block_pool.tile([P, PASSES * P], U8, name=name + "_scale_bytes", align_bytes=64)
+        def quantise(tile, col, mx, name, q, banks):
+            b, r = divmod(q, BLOCK_BANKS)
+            if r == 0:
+                codes_tile = block_pool.tile([P, BLOCK_BANKS * BANK_COLS], U32, name=name + "_codes", align_bytes=64)
+                scale_bytes = block_pool.tile(
+                    [P, BLOCK_BANKS * BANK_COLS], U8, name=name + "_scale_bytes", align_bytes=64
+                )
                 mx[b] = (codes_tile, scale_bytes)
             codes_tile, scale_bytes = mx[b]
-            first = r * BATCH_COLS + ci * BANK_COLS
-            cols = slice(first, first + banks * BANK_COLS)
+            cols = slice(r * BANK_COLS, (r + banks) * BANK_COLS)
             nc.vector.quantize_mx(
                 out=codes_tile[:, cols].bitcast(FP8X4),
                 scales=scale_bytes[:, cols],
-                in_=grouped[t][:, ci * BANK_COLS : (ci + banks) * BANK_COLS, :].rearrange("p m t -> p (m t)"),
+                in_=tile[:, col : col + banks * BANK_COLS, :].rearrange("p m t -> p (m t)"),
             )
 
-        def multiply(t):
-            b, r = divmod(t, BLOCK_BATCHES)
+        def quantise_a(r):
+            banks = round_banks(r)
+            if len(banks) == BATCH_BANKS and banks[0] // BLOCK_BANKS == banks[-1] // BLOCK_BANKS:
+                quantise(a_grouped[r], 0, a_mx, "a", banks[0], BATCH_BANKS)
+            else:
+                for j, q in enumerate(banks):
+                    quantise(a_grouped[r], j * BANK_COLS, a_mx, "a", q, 1)
+
+        def quantise_w(q):
+            t, j = divmod(q, BATCH_BANKS)
+            quantise(w_grouped[t], j * BANK_COLS, w_mx, "w", q, 1)
+
+        def multiply(q):
+            b, r = divmod(q, BLOCK_BANKS)
             a_codes, a_scale_bytes = a_mx[b]
             w_codes, w_scale_bytes = w_mx[b]
             if r == 0:
                 acc = ps_acc.tile([P, OUTS], F32)
                 accs[b] = acc
-            for s in range(r * BATCH_PASSES, (r + 1) * BATCH_PASSES):
+            for s in range(BANK_PASSES * r, BANK_PASSES * (r + 1)):
                 cols = slice(s * P, (s + 1) * P)
                 nc.tensor.matmul_mx(
                     out=accs[b][:],
@@ -251,7 +273,7 @@ def tile_decoder_pa_k_kernel(tc, h6_pre, g6, be6, W7, b7, out):
                     rhs=w_codes[:, cols].bitcast(FP8X4),
                     rhs_scale=w_scale_bytes[:, cols],
                     start=(s == 0),
-                    stop=(s == PASSES - 1),
+                    stop=(s == BANK_PASSES * BLOCK_BANKS - 1),
                 )
 
         def finish(b):
@@ -273,52 +295,62 @@ def tile_decoder_pa_k_kernel(tc, h6_pre, g6, be6, W7, b7, out):
                 load(h_rows, h6_pre, t + 1)
                 load(w_rows, W7, t)
             nc.sync.dma_start(out=bias_all[:], in_=b7.rearrange("b j -> (b j)").partition_broadcast(P))
-            transpose_h(0, 0)
+            transpose_h(0)
             transpose_affine()
-            transpose_h(0, 1)
-            transpose_w(0, 0)
-            for t in range(BATCHES + A_LAG + 1):
+            transpose_h(1)
+            transpose_w(0)
+            for q in range(2, H_BANKS):
+                transpose_h(q)
+            quantised = 0
+            multiplied = 0
+            t = 0
+            while multiplied < BANKS:
                 if live(t + PREFETCH + 1):
                     load(h_rows, h6_pre, t + PREFETCH + 1)
                 if live(t + PREFETCH):
                     load(w_rows, W7, t + PREFETCH)
-                if live(t - A_LAG - 1):
-                    multiply(t - A_LAG - 1)
+                finished = []
+                while multiplied < quantised and not finished:
+                    multiply(multiplied)
+                    multiplied += 1
+                    if multiplied % BLOCK_BANKS == 0:
+                        finished.append(multiplied // BLOCK_BANKS - 1)
                 if live(t):
                     statistics(t)
-                for ci in range(BATCH_BANKS):
-                    if live(t + 1):
-                        transpose_h(t + 1, ci)
-                    for g in range(BANK_PASSES):
-                        if live(t - 1):
-                            activations(t - 1, ci, g)
-                        if live(t) and (ci, g) == (0 if t == 0 else BATCH_BANKS - 1, 0):
-                            spread(t)
-                    w_bank = t * BATCH_BANKS + ci - 1
-                    if 0 <= w_bank < BATCHES * BATCH_BANKS:
-                        copy_w(*divmod(w_bank, BATCH_BANKS))
-                    if 0 <= w_bank < BATCHES * BATCH_BANKS - 1:
-                        transpose_w(*divmod(w_bank + 1, BATCH_BANKS))
-                if live(t - 1) and t - 1 < BATCHES - VECTOR_BATCHES:
-                    regroup(t - 1)
-                for ci in range(BATCH_BANKS):
-                    if live(t - A_LAG) and t - A_LAG < BATCHES - VECTOR_BATCHES and ci == 0:
-                        quantise(a_grouped, a_mx, "a", t - A_LAG, 0, BATCH_BANKS)
-                    if live(t - A_LAG) and t - A_LAG >= BATCHES - VECTOR_BATCHES:
-                        quantise(a_grouped, a_mx, "a", t - A_LAG, ci)
-                    if live(t - A_LAG + 1) and t - A_LAG + 1 >= BATCHES - VECTOR_BATCHES:
-                        regroup_on_vector(t - A_LAG + 1, ci * BANK_COLS, (ci + 1) * BANK_COLS)
+                if t == 0:
+                    spread(0)
+                for j in range(BATCH_BANKS):
+                    w_bank = t * BATCH_BANKS + j - 1
+                    if j < len(round_banks(t)):
+                        activations(t, round_banks(t)[j], 0)
+                    if t > 0 and live(t) and j == BATCH_BANKS - 1:
+                        spread(t)
+                    if j < len(round_banks(t)):
+                        q = round_banks(t)[j]
+                        activations(t, q, 1)
+                        if q + H_BANKS < BANKS:
+                            transpose_h(q + H_BANKS)
+                    if 0 <= w_bank < BANKS:
+                        copy_w(w_bank)
+                        if w_bank + 1 < BANKS:
+                            transpose_w(w_bank + 1)
+                if round_banks(t) and on_gpsimd(t):
+                    regroup(t)
+                if round_banks(t - 2):
+                    quantise_a(t - 2)
+                    quantised = round_banks(t - 2)[-1] + 1
                 if live(t):
                     scale_term(t)
                 if live(t - 1):
-                    quantise(w_grouped, w_mx, "w", t - 1, 0)
+                    quantise_w((t - 1) * BATCH_BANKS)
                 if live(t):
                     scaled_mean(t)
-                if live(t - 2) and t - 2 < BATCHES - VECTOR_BATCHES:
-                    regroup_on_vector(t - 2, GPSIMD_COLS, BATCH_COLS)
+                if round_banks(t - 1):
+                    regroup_on_vector(t - 1, GPSIMD_COLS if on_gpsimd(t - 1) else 0, len(round_banks(t - 1)) * BANK_COLS)
                 if live(t - 1):
-                    quantise(w_grouped, w_mx, "w", t - 1, 1)
+                    quantise_w((t - 1) * BATCH_BANKS + 1)
                 if live(t):
                     shift_term(t)
-                if live(t - A_LAG - 1) and (t - A_LAG - 1) % BLOCK_BATCHES == BLOCK_BATCHES - 1:
-                    finish((t - A_LAG - 1) // BLOCK_BATCHES)
+                for b in finished:
+                    finish(b)
+                t += 1

@@ -33,11 +33,16 @@ H_BANKS = 5
 BATCH_BANKS = 2
 BATCHES = BANKS // BATCH_BANKS
 BATCH_FEATS = BATCH_BANKS * BANK_FEATS
+ROUNDS = BATCHES + 2
 PREFETCH = 6
 BEHIND = 1
 RUN = 4
 GPSIMD_COLS = 464
-VECTOR_ROUNDS = 3
+SCALAR_EVERY = 2
+LAST_ROUNDS = 3
+EARLY_TURNS = 2
+W_BANKS = 2
+LAST_SCALAR_COLS = 128
 
 FLOPS = 2 * BLOCKS * ROWS * OUTS * FEATS
 
@@ -50,7 +55,7 @@ def tile_decoder_pa_k_kernel(tc, h6_pre, g6, be6, W7, b7, out):
         block_pool = ctx.enter_context(tc.tile_pool(name="block_pool", bufs=2))
         work = ctx.enter_context(tc.tile_pool(name="work", bufs=4))
         ps_h = ctx.enter_context(tc.psum_pool(name="ps_h", bufs=H_BANKS))
-        ps_w = ctx.enter_context(tc.psum_pool(name="ps_w", bufs=2))
+        ps_w = ctx.enter_context(tc.psum_pool(name="ps_w", bufs=W_BANKS))
         ps_acc = ctx.enter_context(tc.psum_pool(name="ps_acc", bufs=1))
 
         ident = const.tile([P, P], F32)
@@ -135,17 +140,19 @@ def tile_decoder_pa_k_kernel(tc, h6_pre, g6, be6, W7, b7, out):
             transpose_bank(w_ps, w_rows, q)
             w_banks[q] = w_ps
 
-        def statistics(t):
-            batch_stats = work.tile([P, BATCH_BANKS * BANK_GROUPS, 6], F32)
-            for j in range(BATCH_BANKS):
-                for g in range(BANK_PASSES):
-                    for u in range(PAIR):
-                        quarter = BANK_PASSES * u + g
-                        nc.vector.bn_stats(
-                            out=batch_stats[:, BANK_GROUPS * j + PAIR * g + u, :],
-                            in_=h_banks[t * BATCH_BANKS + j][:, quarter * P : (quarter + 1) * P].bitcast(BF16),
-                        )
-            stats[t] = batch_stats[:].rearrange("p i (e s) -> p s (i e)", s=3)
+        def statistics(q, first=0, last=BANK_GROUPS):
+            t, j = divmod(q, BATCH_BANKS)
+            if t not in stats_tiles:
+                batch_stats = work.tile([P, BATCH_BANKS * BANK_GROUPS, 6], F32)
+                stats_tiles[t] = batch_stats
+                stats[t] = batch_stats[:].rearrange("p i (e s) -> p s (i e)", s=3)
+            for i in range(first, last):
+                g, u = divmod(i, PAIR)
+                quarter = BANK_PASSES * u + g
+                nc.vector.bn_stats(
+                    out=stats_tiles[t][:, BANK_GROUPS * j + i, :],
+                    in_=h_banks[q][:, quarter * P : (quarter + 1) * P].bitcast(BF16),
+                )
 
         def spread(t):
             rstd = work.tile([P, BATCH_FEATS], F32)
@@ -201,7 +208,7 @@ def tile_decoder_pa_k_kernel(tc, h6_pre, g6, be6, W7, b7, out):
                     )
 
         def on_gpsimd(r):
-            return len(round_banks(r)) == BATCH_BANKS and r <= BATCHES + 1 - VECTOR_ROUNDS
+            return len(round_banks(r)) == BATCH_BANKS and r < ROUNDS - LAST_ROUNDS
 
         def regroup(r):
             nc.gpsimd.tensor_scalar(
@@ -213,9 +220,16 @@ def tile_decoder_pa_k_kernel(tc, h6_pre, g6, be6, W7, b7, out):
                 op1=ALU.add,
             )
 
-        def regroup_on_vector(r, first, last):
-            nc.vector.tensor_copy(
-                out=a_grouped[r][:, first:last, :], in_=a_planes[r][:, :, first:last].rearrange("p t c -> p c t")
+        def regroup_cols(copy, r, first, last):
+            copy(out=a_grouped[r][:, first:last, :], in_=a_planes[r][:, :, first:last].rearrange("p t c -> p c t"))
+
+        def regroup_rest(r):
+            on_scalar = on_gpsimd(r) and r % SCALAR_EVERY == 0
+            regroup_cols(
+                nc.scalar.copy if on_scalar else nc.vector.tensor_copy,
+                r,
+                GPSIMD_COLS if on_gpsimd(r) else 0,
+                len(round_banks(r)) * BANK_COLS,
             )
 
         def copy_w(q):
@@ -250,8 +264,11 @@ def tile_decoder_pa_k_kernel(tc, h6_pre, g6, be6, W7, b7, out):
             if len(banks) == BATCH_BANKS and banks[0] // BLOCK_BANKS == banks[-1] // BLOCK_BANKS:
                 quantise(a_grouped[r], 0, a_mx, "a", banks[0], BATCH_BANKS)
             else:
-                for j, q in enumerate(banks):
-                    quantise(a_grouped[r], j * BANK_COLS, a_mx, "a", q, 1)
+                for q in banks:
+                    quantise_a_bank(r, q)
+
+        def quantise_a_bank(r, q):
+            quantise(a_grouped[r], round_banks(r).index(q) * BANK_COLS, a_mx, "a", q, 1)
 
         def quantise_w(q):
             t, j = divmod(q, BATCH_BANKS)
@@ -281,6 +298,19 @@ def tile_decoder_pa_k_kernel(tc, h6_pre, g6, be6, W7, b7, out):
             nc.vector.tensor_add(out=result[:], in0=accs[b][:], in1=bias_all[:, b * OUTS : (b + 1) * OUTS])
             nc.sync.dma_start(out=out[b], in_=result[:])
 
+        def activate_bank(r, q):
+            for g in range(BANK_PASSES):
+                activations(r, q, g)
+                if g == 0 and round_banks(r).index(q) == BATCH_BANKS - 1 and live(r):
+                    spread(r)
+            if q + H_BANKS < BANKS:
+                transpose_h(q + H_BANKS)
+
+        def empty_w(q):
+            copy_w(q)
+            if q + W_BANKS < BANKS:
+                transpose_w(q + W_BANKS)
+
         def live(t):
             return 0 <= t < BATCHES
 
@@ -288,8 +318,9 @@ def tile_decoder_pa_k_kernel(tc, h6_pre, g6, be6, W7, b7, out):
             load(h_rows, h6_pre, 0, 0, BATCH_BANKS)
             load_affine()
             load(h_rows, h6_pre, 0, 1, BATCH_BANKS)
+            load(h_rows, h6_pre, 1, 0, BATCH_BANKS)
             load(w_rows, W7, 0, 0, BATCH_BANKS)
-            load(h_rows, h6_pre, 1)
+            load(h_rows, h6_pre, 1, 1, BATCH_BANKS)
             load(w_rows, W7, 0, 1, BATCH_BANKS)
             for t in range(1, PREFETCH):
                 load(h_rows, h6_pre, t + 1)
@@ -298,13 +329,15 @@ def tile_decoder_pa_k_kernel(tc, h6_pre, g6, be6, W7, b7, out):
             transpose_h(0)
             transpose_affine()
             transpose_h(1)
+            transpose_h(2)
             transpose_w(0)
-            for q in range(2, H_BANKS):
-                transpose_h(q)
+            transpose_h(3)
+            transpose_w(1)
+            transpose_h(4)
+            counted = 0
             quantised = 0
             multiplied = 0
-            t = 0
-            while multiplied < BANKS:
+            for t in range(BATCHES):
                 if live(t + PREFETCH + 1):
                     load(h_rows, h6_pre, t + PREFETCH + 1)
                 if live(t + PREFETCH):
@@ -315,42 +348,70 @@ def tile_decoder_pa_k_kernel(tc, h6_pre, g6, be6, W7, b7, out):
                     multiplied += 1
                     if multiplied % BLOCK_BANKS == 0:
                         finished.append(multiplied // BLOCK_BANKS - 1)
-                if live(t):
-                    statistics(t)
+                while counted < (t + 1) * BATCH_BANKS:
+                    statistics(counted)
+                    counted += 1
+                early = counted if t < EARLY_TURNS else None
+                if early is not None:
+                    counted += 1
                 if t == 0:
                     spread(0)
                 for j in range(BATCH_BANKS):
+                    if j < len(round_banks(t)):
+                        activate_bank(t, round_banks(t)[j])
                     w_bank = t * BATCH_BANKS + j - 1
-                    if j < len(round_banks(t)):
-                        activations(t, round_banks(t)[j], 0)
-                    if t > 0 and live(t) and j == BATCH_BANKS - 1:
+                    if w_bank >= 0:
+                        empty_w(w_bank)
+                    if j == 0 and len(round_banks(t)) == 1:
                         spread(t)
-                    if j < len(round_banks(t)):
-                        q = round_banks(t)[j]
-                        activations(t, q, 1)
-                        if q + H_BANKS < BANKS:
-                            transpose_h(q + H_BANKS)
-                    if 0 <= w_bank < BANKS:
-                        copy_w(w_bank)
-                        if w_bank + 1 < BANKS:
-                            transpose_w(w_bank + 1)
-                if round_banks(t) and on_gpsimd(t):
+                if on_gpsimd(t):
                     regroup(t)
+                for b in finished:
+                    finish(b)
                 if round_banks(t - 2):
                     quantise_a(t - 2)
                     quantised = round_banks(t - 2)[-1] + 1
-                if live(t):
-                    scale_term(t)
+                if round_banks(t - 1):
+                    regroup_rest(t - 1)
+                if early is not None:
+                    statistics(early, 0, 2)
+                scale_term(t)
                 if live(t - 1):
                     quantise_w((t - 1) * BATCH_BANKS)
-                if live(t):
-                    scaled_mean(t)
-                if round_banks(t - 1):
-                    regroup_on_vector(t - 1, GPSIMD_COLS if on_gpsimd(t - 1) else 0, len(round_banks(t - 1)) * BANK_COLS)
+                if early is not None:
+                    statistics(early, 2, 3)
+                scaled_mean(t)
                 if live(t - 1):
                     quantise_w((t - 1) * BATCH_BANKS + 1)
-                if live(t):
-                    shift_term(t)
-                for b in finished:
-                    finish(b)
-                t += 1
+                if early is not None:
+                    statistics(early, 3, 4)
+                shift_term(t)
+
+            r0, r1, r2, r3 = range(BATCHES - 2, BATCHES + 2)
+            second_last, last = round_banks(r2)
+            final_bank = round_banks(r3)[0]
+            while multiplied < quantised:
+                multiply(multiplied)
+                multiplied += 1
+                if multiplied % BLOCK_BANKS == 0:
+                    finish(multiplied // BLOCK_BANKS - 1)
+            activate_bank(r2, second_last)
+            empty_w(BANKS - 1)
+            activate_bank(r2, last)
+            activate_bank(r3, final_bank)
+            regroup_rest(r1)
+            quantise_a(r0)
+            quantise_w(BANKS - 2)
+            regroup_cols(nc.vector.tensor_copy, r2, 0, BANK_COLS)
+            quantise_a(r1)
+            regroup_cols(nc.vector.tensor_copy, r2, BANK_COLS, 2 * BANK_COLS)
+            quantise_a_bank(r2, second_last)
+            quantise_w(BANKS - 1)
+            regroup_cols(nc.scalar.copy, r3, 0, LAST_SCALAR_COLS)
+            regroup_cols(nc.vector.tensor_copy, r3, LAST_SCALAR_COLS, BANK_COLS)
+            quantise_a_bank(r2, last)
+            for q in range(multiplied, final_bank):
+                multiply(q)
+            quantise_a_bank(r3, final_bank)
+            multiply(final_bank)
+            finish(BLOCKS - 1)

from contextlib import ExitStack

import concourse.mybir as mybir
from concourse.masks import make_identity

F32 = mybir.dt.float32
BF16 = mybir.dt.bfloat16
U32 = mybir.dt.uint32
U8 = mybir.dt.uint8
FP8X4 = mybir.dt.float8_e4m3fn_x4
ACT = mybir.ActivationFunctionType
ALU = mybir.AluOpType

P = 128
BLOCKS = 8
ROWS = 128
FEATS = 8192
OUTS = 128
EPS = 1e-5

PACK = 4
PAIR = 2
GROUP_K = P * PAIR
K_PASS = P * PACK
BANK_GROUPS = 4
BANK_PASSES = 2
BANK_K = BANK_GROUPS * GROUP_K
BANK_FEATS = BANK_GROUPS * PAIR
BANK_COLS = BANK_PASSES * ROWS
BLOCK_BANKS = FEATS // BANK_K
BANKS = BLOCKS * BLOCK_BANKS
H_BANKS = 5
BATCH_BANKS = 2
BATCHES = BANKS // BATCH_BANKS
BATCH_FEATS = BATCH_BANKS * BANK_FEATS
ROUNDS = BATCHES + 2
PREFETCH = 6
BEHIND = 1
RUN = 4
GPSIMD_COLS = 464
SCALAR_EVERY = 2
LAST_ROUNDS = 3
EARLY_TURNS = 2
W_BANKS = 2
LAST_SCALAR_COLS = 128

FLOPS = 2 * BLOCKS * ROWS * OUTS * FEATS


def tile_decoder_pa_k_kernel(tc, h6_pre, g6, be6, W7, b7, out):
    nc = tc.nc
    with ExitStack() as ctx:
        const = ctx.enter_context(tc.tile_pool(name="const", bufs=1))
        rows_pool = ctx.enter_context(tc.tile_pool(name="rows_pool", bufs=2 * PREFETCH + 5))
        block_pool = ctx.enter_context(tc.tile_pool(name="block_pool", bufs=2))
        work = ctx.enter_context(tc.tile_pool(name="work", bufs=4))
        ps_h = ctx.enter_context(tc.psum_pool(name="ps_h", bufs=H_BANKS))
        ps_w = ctx.enter_context(tc.psum_pool(name="ps_w", bufs=W_BANKS))
        ps_acc = ctx.enter_context(tc.psum_pool(name="ps_acc", bufs=1))

        ident = const.tile([P, P], F32)
        make_identity(nc, ident[:])
        zero_col = const.tile([P, 1], F32)
        nc.vector.memset(zero_col[:], 0.0)
        eps_col = const.tile([P, 1], F32)
        nc.vector.tensor_scalar(out=eps_col[:], in0=zero_col[:], scalar1=1.0, scalar2=EPS, op0=ALU.mult, op1=ALU.add)
        warm_col = const.tile([P, 1], F32)
        nc.scalar.activation(out=warm_col[:], in_=zero_col[:], func=ACT.Abs_reciprocal_sqrt, bias=eps_col[:])

        bias_all = const.tile([P, BLOCKS * OUTS], BF16)
        affine = const.tile([P, 2, BANKS * BANK_FEATS], F32)
        vec_rows = []

        h_rows = {}
        w_rows = {}
        h_banks = {}
        w_banks = {}
        stats_tiles = {}
        stats = {}
        rstds = {}
        means_scaled = {}
        scales = {}
        shifts = {}
        a_planes = {}
        a_grouped = {}
        w_grouped = {}
        a_mx = {}
        w_mx = {}
        accs = {}

        def load(rows, source, i, part=0, parts=1):
            if part == 0:
                rows_tile = rows_pool.tile([P, BATCH_BANKS * BANK_K], BF16)
                rows[i] = rows_tile
            b, r = divmod(i * BATCH_BANKS, BLOCK_BANKS)
            first, last = (part * BATCH_BANKS * BANK_K // parts, (part + 1) * BATCH_BANKS * BANK_K // parts)
            nc.sync.dma_start(
                out=rows[i][:, first:last], in_=source[b][:, r * BANK_K + first : r * BANK_K + last]
            )

        def transpose_bank(bank, rows, q):
            i, part = divmod(q, BATCH_BANKS)
            words = rows[i][:, part * BANK_K : (part + 1) * BANK_K].bitcast(F32)
            for g in range(BANK_PASSES):
                for u in range(PAIR):
                    quarter = BANK_PASSES * u + g
                    nc.tensor.transpose(
                        bank[:, quarter * P : (quarter + 1) * P],
                        words[:, g * GROUP_K + u : (g + 1) * GROUP_K : PAIR],
                        ident[:],
                    )

        def load_affine():
            for v, vec in enumerate((g6, be6)):
                rows_tile = const.tile([P, K_PASS], BF16, name="vec_rows%d" % v)
                nc.sync.dma_start(out=rows_tile[:], in_=vec.rearrange("b (s w) -> (b s) w", w=K_PASS))
                vec_rows.append(rows_tile)

        def transpose_affine():
            affine_ps = ps_w.tile([P, BANK_GROUPS * P], F32, tag="w_ps")
            for v in range(2):
                for u in range(PAIR):
                    quarter = PAIR * v + u
                    nc.tensor.transpose(
                        affine_ps[:, quarter * P : (quarter + 1) * P], vec_rows[v][:].bitcast(F32)[:, u::PAIR], ident[:]
                    )
            for v in range(2):
                nc.scalar.copy(
                    out=affine[:, v, :].rearrange("p (s u e) -> p s u e", u=PAIR, e=PAIR),
                    in_=affine_ps[:].bitcast(BF16).rearrange("p (v u s e) -> p v s u e", v=2, u=PAIR, e=PAIR)[:, v],
                )

        def transpose_h(q):
            h_ps = ps_h.tile([P, BANK_GROUPS * P], F32)
            transpose_bank(h_ps, h_rows, q)
            h_banks[q] = h_ps

        def transpose_w(q):
            w_ps = ps_w.tile([P, BANK_GROUPS * P], F32)
            transpose_bank(w_ps, w_rows, q)
            w_banks[q] = w_ps

        def statistics(q, first=0, last=BANK_GROUPS):
            t, j = divmod(q, BATCH_BANKS)
            if t not in stats_tiles:
                batch_stats = work.tile([P, BATCH_BANKS * BANK_GROUPS, 6], F32)
                stats_tiles[t] = batch_stats
                stats[t] = batch_stats[:].rearrange("p i (e s) -> p s (i e)", s=3)
            for i in range(first, last):
                g, u = divmod(i, PAIR)
                quarter = BANK_PASSES * u + g
                nc.vector.bn_stats(
                    out=stats_tiles[t][:, BANK_GROUPS * j + i, :],
                    in_=h_banks[q][:, quarter * P : (quarter + 1) * P].bitcast(BF16),
                )

        def spread(t):
            rstd = work.tile([P, BATCH_FEATS], F32)
            nc.scalar.activation(
                out=rstd[:],
                in_=stats[t][:, 2, :],
                func=ACT.Abs_reciprocal_sqrt,
                scale=1.0 / ROWS,
                bias=eps_col[:],
            )
            rstds[t] = rstd

        def batch_feats(t):
            return slice(t * BATCH_FEATS, (t + 1) * BATCH_FEATS)

        def scale_term(t):
            scale = work.tile([P, BATCH_FEATS], F32)
            nc.vector.tensor_mul(out=scale[:], in0=rstds[t][:], in1=affine[:, 0, batch_feats(t)])
            scales[t] = scale

        def scaled_mean(t):
            mean_scaled = work.tile([P, BATCH_FEATS], F32)
            nc.vector.tensor_mul(out=mean_scaled[:], in0=stats[t][:, 1, :], in1=scales[t][:])
            means_scaled[t] = mean_scaled

        def shift_term(t):
            shift = work.tile([P, BATCH_FEATS], F32)
            nc.vector.tensor_sub(out=shift[:], in0=affine[:, 1, batch_feats(t)], in1=means_scaled[t][:])
            shifts[t] = shift

        def round_banks(r):
            first = (r - 1) * BATCH_BANKS - BEHIND
            return [q for q in range(first, first + BATCH_BANKS) if 0 <= q < BANKS]

        def activations(r, q, g):
            if q == round_banks(r)[0] and g == 0:
                planes_tile = work.tile([P, PACK, BATCH_BANKS * BANK_COLS], BF16)
                a_planes[r] = planes_tile
                a_grouped_tile = work.tile([P, BATCH_BANKS * BANK_COLS, PACK], BF16, align_bytes=64)
                a_grouped[r] = a_grouped_tile
            t, j = divmod(q, BATCH_BANKS)
            halves = h_banks[q][:].bitcast(BF16).rearrange("p (u g n e) -> p u g n e", u=PAIR, g=BANK_PASSES, e=PAIR)
            first = round_banks(r).index(q) * BANK_COLS + g * ROWS
            for u in range(PAIR):
                for e in range(PAIR):
                    col = BANK_FEATS * j + PACK * g + PAIR * u + e
                    nc.scalar.activation(
                        out=a_planes[r][:, PAIR * u + e, first : first + ROWS],
                        in_=halves[:, u, g, :, e],
                        func=ACT.Relu,
                        scale=scales[t][:, col : col + 1],
                        bias=shifts[t][:, col : col + 1],
                    )

        def on_gpsimd(r):
            return len(round_banks(r)) == BATCH_BANKS and r < ROUNDS - LAST_ROUNDS

        def regroup(r):
            nc.gpsimd.tensor_scalar(
                out=a_grouped[r][:, :GPSIMD_COLS, :].rearrange("p (c i) t -> p c t i", i=RUN),
                in0=a_planes[r][:, :, :GPSIMD_COLS].rearrange("p t (c i) -> p c t i", i=RUN),
                scalar1=1.0,
                scalar2=0.0,
                op0=ALU.mult,
                op1=ALU.add,
            )

        def regroup_cols(copy, r, first, last):
            copy(out=a_grouped[r][:, first:last, :], in_=a_planes[r][:, :, first:last].rearrange("p t c -> p c t"))

        def regroup_rest(r):
            on_scalar = on_gpsimd(r) and r % SCALAR_EVERY == 0
            regroup_cols(
                nc.scalar.copy if on_scalar else nc.vector.tensor_copy,
                r,
                GPSIMD_COLS if on_gpsimd(r) else 0,
                len(round_banks(r)) * BANK_COLS,
            )

        def copy_w(q):
            t, j = divmod(q, BATCH_BANKS)
            if j == 0:
                w_grouped_tile = work.tile([P, BATCH_BANKS * BANK_COLS, PACK], BF16, align_bytes=64)
                w_grouped[t] = w_grouped_tile
            part = w_grouped[t][:, j * BANK_COLS : (j + 1) * BANK_COLS, :]
            nc.scalar.copy(
                out=part.rearrange("p m t -> p (m t)").bitcast(F32).rearrange("p (m u) -> p m u", u=PAIR),
                in_=w_banks[q][:].rearrange("p (u m) -> p m u", u=PAIR),
            )

        def quantise(tile, col, mx, name, q, banks):
            b, r = divmod(q, BLOCK_BANKS)
            if r == 0:
                codes_tile = block_pool.tile([P, BLOCK_BANKS * BANK_COLS], U32, name=name + "_codes", align_bytes=64)
                scale_bytes = block_pool.tile(
                    [P, BLOCK_BANKS * BANK_COLS], U8, name=name + "_scale_bytes", align_bytes=64
                )
                mx[b] = (codes_tile, scale_bytes)
            codes_tile, scale_bytes = mx[b]
            cols = slice(r * BANK_COLS, (r + banks) * BANK_COLS)
            nc.vector.quantize_mx(
                out=codes_tile[:, cols].bitcast(FP8X4),
                scales=scale_bytes[:, cols],
                in_=tile[:, col : col + banks * BANK_COLS, :].rearrange("p m t -> p (m t)"),
            )

        def quantise_a(r):
            banks = round_banks(r)
            if len(banks) == BATCH_BANKS and banks[0] // BLOCK_BANKS == banks[-1] // BLOCK_BANKS:
                quantise(a_grouped[r], 0, a_mx, "a", banks[0], BATCH_BANKS)
            else:
                for q in banks:
                    quantise_a_bank(r, q)

        def quantise_a_bank(r, q):
            quantise(a_grouped[r], round_banks(r).index(q) * BANK_COLS, a_mx, "a", q, 1)

        def quantise_w(q):
            t, j = divmod(q, BATCH_BANKS)
            quantise(w_grouped[t], j * BANK_COLS, w_mx, "w", q, 1)

        def multiply(q):
            b, r = divmod(q, BLOCK_BANKS)
            a_codes, a_scale_bytes = a_mx[b]
            w_codes, w_scale_bytes = w_mx[b]
            if r == 0:
                acc = ps_acc.tile([P, OUTS], F32)
                accs[b] = acc
            for s in range(BANK_PASSES * r, BANK_PASSES * (r + 1)):
                cols = slice(s * P, (s + 1) * P)
                nc.tensor.matmul_mx(
                    out=accs[b][:],
                    lhsT=a_codes[:, cols].bitcast(FP8X4),
                    lhsT_scale=a_scale_bytes[:, cols],
                    rhs=w_codes[:, cols].bitcast(FP8X4),
                    rhs_scale=w_scale_bytes[:, cols],
                    start=(s == 0),
                    stop=(s == BANK_PASSES * BLOCK_BANKS - 1),
                )

        def finish(b):
            result = work.tile([P, OUTS], F32)
            nc.vector.tensor_add(out=result[:], in0=accs[b][:], in1=bias_all[:, b * OUTS : (b + 1) * OUTS])
            nc.sync.dma_start(out=out[b], in_=result[:])

        def activate_bank(r, q):
            for g in range(BANK_PASSES):
                activations(r, q, g)
                if g == 0 and round_banks(r).index(q) == BATCH_BANKS - 1 and live(r):
                    spread(r)
            if q + H_BANKS < BANKS:
                transpose_h(q + H_BANKS)

        def empty_w(q):
            copy_w(q)
            if q + W_BANKS < BANKS:
                transpose_w(q + W_BANKS)

        def live(t):
            return 0 <= t < BATCHES

        with tc.manual_schedule():
            load(h_rows, h6_pre, 0, 0, BATCH_BANKS)
            load_affine()
            load(h_rows, h6_pre, 0, 1, BATCH_BANKS)
            load(h_rows, h6_pre, 1, 0, BATCH_BANKS)
            load(w_rows, W7, 0, 0, BATCH_BANKS)
            load(h_rows, h6_pre, 1, 1, BATCH_BANKS)
            load(w_rows, W7, 0, 1, BATCH_BANKS)
            for t in range(1, PREFETCH):
                load(h_rows, h6_pre, t + 1)
                load(w_rows, W7, t)
            nc.sync.dma_start(out=bias_all[:], in_=b7.rearrange("b j -> (b j)").partition_broadcast(P))
            transpose_h(0)
            transpose_affine()
            transpose_h(1)
            transpose_h(2)
            transpose_w(0)
            transpose_h(3)
            transpose_w(1)
            transpose_h(4)
            counted = 0
            quantised = 0
            multiplied = 0
            for t in range(BATCHES):
                if live(t + PREFETCH + 1):
                    load(h_rows, h6_pre, t + PREFETCH + 1)
                if live(t + PREFETCH):
                    load(w_rows, W7, t + PREFETCH)
                finished = []
                while multiplied < quantised and not finished:
                    multiply(multiplied)
                    multiplied += 1
                    if multiplied % BLOCK_BANKS == 0:
                        finished.append(multiplied // BLOCK_BANKS - 1)
                while counted < (t + 1) * BATCH_BANKS:
                    statistics(counted)
                    counted += 1
                early = counted if t < EARLY_TURNS else None
                if early is not None:
                    counted += 1
                if t == 0:
                    spread(0)
                for j in range(BATCH_BANKS):
                    if j < len(round_banks(t)):
                        activate_bank(t, round_banks(t)[j])
                    w_bank = t * BATCH_BANKS + j - 1
                    if w_bank >= 0:
                        empty_w(w_bank)
                    if j == 0 and len(round_banks(t)) == 1:
                        spread(t)
                if on_gpsimd(t):
                    regroup(t)
                for b in finished:
                    finish(b)
                if round_banks(t - 2):
                    quantise_a(t - 2)
                    quantised = round_banks(t - 2)[-1] + 1
                if round_banks(t - 1):
                    regroup_rest(t - 1)
                if early is not None:
                    statistics(early, 0, 2)
                scale_term(t)
                if live(t - 1):
                    quantise_w((t - 1) * BATCH_BANKS)
                if early is not None:
                    statistics(early, 2, 3)
                scaled_mean(t)
                if live(t - 1):
                    quantise_w((t - 1) * BATCH_BANKS + 1)
                if early is not None:
                    statistics(early, 3, 4)
                shift_term(t)

            r0, r1, r2, r3 = range(BATCHES - 2, BATCHES + 2)
            second_last, last = round_banks(r2)
            final_bank = round_banks(r3)[0]
            while multiplied < quantised:
                multiply(multiplied)
                multiplied += 1
                if multiplied % BLOCK_BANKS == 0:
                    finish(multiplied // BLOCK_BANKS - 1)
            activate_bank(r2, second_last)
            empty_w(BANKS - 1)
            activate_bank(r2, last)
            activate_bank(r3, final_bank)
            regroup_rest(r1)
            quantise_a(r0)
            quantise_w(BANKS - 2)
            regroup_cols(nc.vector.tensor_copy, r2, 0, BANK_COLS)
            quantise_a(r1)
            regroup_cols(nc.vector.tensor_copy, r2, BANK_COLS, 2 * BANK_COLS)
            quantise_a_bank(r2, second_last)
            quantise_w(BANKS - 1)
            regroup_cols(nc.scalar.copy, r3, 0, LAST_SCALAR_COLS)
            regroup_cols(nc.vector.tensor_copy, r3, LAST_SCALAR_COLS, BANK_COLS)
            quantise_a_bank(r2, last)
            for q in range(multiplied, final_bank):
                multiply(q)
            quantise_a_bank(r3, final_bank)
            multiply(final_bank)
            finish(BLOCKS - 1)
